import numpy as np
import ml_dtypes


def mxq(x, axis, fmt="e4m3"):
    dtype, down = {"e4m3": (ml_dtypes.float8_e4m3fn, 7), "e5m2": (ml_dtypes.float8_e5m2, 14)}[fmt]
    v = np.moveaxis(np.asarray(x, np.float32).astype(ml_dtypes.bfloat16).astype(np.float64), axis, -1)
    blocks = v.reshape(v.shape[:-1] + (-1, 32))
    amax = np.abs(blocks).max(-1, keepdims=True)
    byte = np.maximum(np.where(amax > 0, np.frexp(amax)[1] - 1 + 127, 0) - down, 1)
    scale = np.exp2(byte - 127.0)
    codes = (blocks / scale).astype(np.float32).astype(dtype).astype(np.float64)
    return np.moveaxis((codes * scale).reshape(v.shape), -1, axis)


WIDE = False


def mx_kscale(k):
    if not WIDE:
        return np.ones(k)
    levels = np.array([10, -10, 5, -5, 0])
    if k % 512:
        return np.exp2(np.random.permutation(np.resize(levels, k // 32))).repeat(32)
    a = np.empty((k // 512, 16))
    for p in range(k // 512):
        a[p, :8] = np.random.permutation(np.resize(levels, 8))
        for g in range(8):
            far = levels[np.abs(levels - a[p, g]) >= 10]
            a[p, g + 8] = far[np.random.randint(len(far))]
    return np.exp2(a.ravel()).repeat(32)


BF16 = ml_dtypes.bfloat16


def bf(x):
    return np.asarray(x, np.float32).astype(BF16)


def f64(x):
    return np.asarray(x).astype(np.float64)


B, S, DIM, QK, EXP, V, G = 16, 1024, 512, 32, 32, 16, 512
W = 2 * QK + 2 * EXP
EPS = 1e-5
ERF_TERMS = 100


def erf(z):
    a = np.minimum(np.abs(z), 6.0)
    a2 = 2.0 * a * a
    term = a.copy()
    tot = a.copy()
    for n in range(1, ERF_TERMS):
        term *= a2
        term /= 2 * n + 1
        tot += term
    return np.sign(z) * 2.0 / np.sqrt(np.pi) * np.exp(-a * a) * tot


def gelu_erf(v):
    return 0.5 * v * (1.0 + erf(v / np.sqrt(2.0)))


def setup_inputs():
    s = mx_kscale(DIM)
    rows = np.exp2(np.random.uniform(-8.0, 1.0, (B, S, 1)))
    off = 0.5 * np.random.standard_normal((B, S, 1))
    gain = np.where(np.arange(W) < 2 * QK, 1.5, 1.0)[:, None]
    return {"x": bf((np.random.standard_normal((B, S, DIM)) + off) * rows),
            "norm_w": bf((1.0 + 0.1 * np.random.standard_normal(DIM)) * s),
            "expand_w": bf(np.random.standard_normal((W, DIM)) * gain / np.sqrt(DIM) / s)}


def reference(x, norm_w, expand_w):
    x = f64(x)
    mu = x.mean(-1, keepdims=True)
    var = ((x - mu) ** 2).mean(-1, keepdims=True)
    h = (x - mu) * (1.0 / np.sqrt(var + EPS)) * f64(norm_w)
    proj = mxq(h, 2, "e4m3") @ mxq(f64(expand_w), 1, "e4m3").T
    q = proj[..., :QK]
    k = proj[..., QK:2 * QK]
    lin = proj[..., 2 * QK:2 * QK + EXP]
    pre = proj[..., 2 * QK + EXP:]
    geglu = lin * gelu_erf(pre)
    return q, k, geglu[..., :EXP - V], geglu[..., EXP - V:]

@@ -1,0 +1,262 @@
+from contextlib import ExitStack
+
+import concourse.mybir as mybir
+from concourse.masks import make_identity
+
+F32 = mybir.dt.float32
+BF16 = mybir.dt.bfloat16
+U32 = mybir.dt.uint32
+U8 = mybir.dt.uint8
+FP8X4 = mybir.dt.float8_e4m3fn_x4
+ALU = mybir.AluOpType
+ACT = mybir.ActivationFunctionType
+
+P = 128
+PACK = 4
+RUN = 8
+TOKENS = 16 * 1024
+DIM = 512
+QK = 32
+EXP = 32
+HALF_EXP = 16
+WIDTH = 2 * QK + 2 * EXP
+EPS = 1e-5
+TILES = TOKENS // P
+QUAD = 4
+QUADS = TILES // QUAD
+
+FLOPS = 2 * TOKENS * DIM * WIDTH
+
+
+def by_slot(row):
+    return row.rearrange("p (b j r) -> p j b r", j=PACK, r=RUN)
+
+
+def slots(row):
+    return row.rearrange("p (j b r) -> p j b r", j=PACK, r=RUN)
+
+
+def turn_rows(nc, turned, rows, identity):
+    for j in range(PACK):
+        nc.tensor.transpose(turned[:, j, :], rows[:, j * P : (j + 1) * P], identity)
+
+
+def tile_latentattentionblock_pa_t_kernel(tc, x, norm_w, expand_w, out_0, out_1, out_2, out_3):
+    nc = tc.nc
+    x_rows = x.flatten_outer_dims().rearrange("(p i) d -> p i d", p=P)
+    q_rows = out_0.flatten_outer_dims().rearrange("(p i) c -> p i c", p=P)
+    k_rows = out_1.flatten_outer_dims().rearrange("(p i) c -> p i c", p=P)
+    gl_rows = out_2.flatten_outer_dims().rearrange("(p i) c -> p i c", p=P)
+    gv_rows = out_3.flatten_outer_dims().rearrange("(p i) c -> p i c", p=P)
+
+    with ExitStack() as ctx:
+        const = ctx.enter_context(tc.tile_pool(name="const", bufs=1))
+        x_pool = ctx.enter_context(tc.tile_pool(name="x", bufs=QUADS))
+        stat_pool = ctx.enter_context(tc.tile_pool(name="stat", bufs=6))
+        unread_pool = ctx.enter_context(tc.tile_pool(name="unread", bufs=6))
+        y_pool = ctx.enter_context(tc.tile_pool(name="y", bufs=8))
+        mx_pool = ctx.enter_context(tc.tile_pool(name="mx", bufs=3))
+        out_pool = ctx.enter_context(tc.tile_pool(name="out", bufs=4))
+        turned_pool = ctx.enter_context(tc.psum_pool(name="turned", bufs=6))
+        proj_pool = ctx.enter_context(tc.psum_pool(name="proj", bufs=2))
+
+        w_rows = const.tile([P, DIM], BF16)
+        nc.scalar.dma_start(out=w_rows[:], in_=expand_w)
+        gain_rows = const.tile([P, P], BF16)
+        nc.vector.memset(gain_rows[:], 0.0)
+        nc.scalar.dma_start(out=gain_rows[0:PACK, :].rearrange("j (b r) -> j b r", r=RUN), in_=norm_w.rearrange("(b j r) -> j b r", j=PACK, r=RUN))
+        x_quads = []
+        for q in range(QUADS):
+            x_quad = x_pool.tile([P, QUAD, DIM], BF16)
+            nc.sync.dma_start(out=x_quad[:], in_=x_rows[:, q * QUAD : (q + 1) * QUAD, :])
+            x_quads.append(x_quad)
+
+        identity = const.tile([P, P], F32)
+        make_identity(nc, identity[:])
+        minus_half = const.tile([P, QUAD], F32)
+        nc.vector.memset(minus_half[:], -0.5)
+
+        gain_rows_f = const.tile([P, P], F32)
+        nc.vector.tensor_copy(out=gain_rows_f[:], in_=gain_rows[:])
+        gain_turned = turned_pool.tile([P, PACK, P], F32, tag="turned")
+        nc.tensor.transpose(gain_turned[:, 0, :], gain_rows_f[:], identity[:])
+        gain = const.tile([P, PACK], F32)
+        nc.vector.tensor_copy(out=gain[:], in_=gain_turned[:, 0, 0:PACK])
+
+        w_rows_f = const.tile([P, DIM], F32)
+        nc.vector.tensor_copy(out=slots(w_rows_f[:]), in_=by_slot(w_rows[:]))
+        w_turned = turned_pool.tile([P, PACK, P], F32, tag="turned")
+        turn_rows(nc, w_turned, w_rows_f, identity[:])
+        w_grouped = const.tile([P, P, PACK], BF16, align_bytes=64)
+        nc.vector.tensor_copy(out=w_grouped[:], in_=w_turned[:].rearrange("p j r -> p r j"))
+        w_codes = const.tile([P, WIDTH], U32, align_bytes=64)
+        w_scales = const.tile([P, WIDTH], U8, align_bytes=64)
+        nc.vector.quantize_mx(
+            out=w_codes[:].bitcast(FP8X4),
+            scales=w_scales[:],
+            in_=w_grouped[:].rearrange("p r j -> p (r j)"),
+        )
+
+        minus_means = {}
+        square_sums = {}
+        rstds = {}
+        turneds = {}
+        groupeds = {}
+        words = {}
+        projs = {}
+        gelus = {}
+
+        def sums(q):
+            if not 0 <= q < QUADS:
+                return
+            by_vector = stat_pool.tile([P, QUAD // 2], F32)
+            by_scalar = stat_pool.tile([P, QUAD // 2], F32)
+            for i in range(QUAD // 2):
+                unread_v = unread_pool.tile([P, DIM], BF16)
+                nc.vector.tensor_scalar(
+                    out=unread_v[:],
+                    in0=x_quads[q][:, i, :],
+                    scalar1=-1.0 / DIM,
+                    scalar2=None,
+                    op0=ALU.mult,
+                    op1=ALU.add,
+                    accum_out=by_vector[:, i : i + 1],
+                )
+                minus_means[(q, i)] = by_vector[:, i : i + 1]
+                unread_s = unread_pool.tile([P, DIM], BF16)
+                nc.scalar.activation(
+                    out=unread_s[:],
+                    in_=x_quads[q][:, QUAD // 2 + i, :],
+                    func=ACT.Identity,
+                    scale=-1.0 / DIM,
+                    accum_out=by_scalar[:, i : i + 1],
+                )
+                minus_means[(q, QUAD // 2 + i)] = by_scalar[:, i : i + 1]
+
+        def squares(q):
+            if not 0 <= q < QUADS:
+                return
+            square_sum = stat_pool.tile([P, QUAD], F32)
+            for i in list(range(QUAD // 2, QUAD)) + list(range(QUAD // 2)):
+                unread_s = unread_pool.tile([P, DIM], BF16)
+                nc.scalar.activation(
+                    out=unread_s[:],
+                    in_=x_quads[q][:, i, :],
+                    func=ACT.Square,
+                    bias=minus_means[(q, i)],
+                    accum_out=square_sum[:, i : i + 1],
+                )
+            square_sums[q] = square_sum
+
+        def inverse_std(q):
+            if not 0 <= q < QUADS:
+                return
+            var_eps = stat_pool.tile([P, QUAD], F32)
+            nc.vector.tensor_scalar(
+                out=var_eps[:], in0=square_sums[q][:], scalar1=1.0 / DIM, scalar2=EPS, op0=ALU.mult, op1=ALU.add
+            )
+            rstd = stat_pool.tile([P, QUAD], F32)
+            nc.gpsimd.tensor_tensor(out=rstd[:], in0=var_eps[:], in1=minus_half[:], op=ALU.pow)
+            rstds[q] = rstd
+
+        def normalise(q):
+            if not 0 <= q < QUADS:
+                return
+            for i in range(QUAD):
+                y = y_pool.tile([P, DIM], F32)
+                engine = nc.gpsimd if i % 2 == 0 else nc.vector
+                engine.tensor_scalar(
+                    out=slots(y[:]),
+                    in0=by_slot(x_quads[q][:, i, :]),
+                    scalar1=minus_means[(q, i)],
+                    scalar2=rstds[q][:, i : i + 1],
+                    op0=ALU.add,
+                    op1=ALU.mult,
+                )
+                turned = turned_pool.tile([P, PACK, P], F32, tag="turned")
+                turn_rows(nc, turned, y, identity[:])
+                turneds[(q, i)] = turned
+
+        def apply_gain(q):
+            if not 0 <= q < QUADS:
+                return
+            grouped = mx_pool.tile([P, QUAD, P, PACK], BF16, align_bytes=64)
+            for i in range(QUAD):
+                nc.vector.tensor_tensor(
+                    out=grouped[:, i, :, :],
+                    in0=turneds[(q, i)][:].rearrange("p j r -> p r j"),
+                    in1=gain[:].unsqueeze(1).to_broadcast([P, P, PACK]),
+                    op=ALU.mult,
+                )
+            groupeds[q] = grouped
+
+        def quantise(q):
+            if not 0 <= q < QUADS:
+                return
+            codes = mx_pool.tile([P, QUAD * P], U32, align_bytes=64)
+            scales = mx_pool.tile([P, QUAD * P], U8, align_bytes=64)
+            nc.vector.quantize_mx(
+                out=codes[:].bitcast(FP8X4),
+                scales=scales[:],
+                in_=groupeds[q][:].rearrange("p i r j -> p (i r j)"),
+            )
+            words[q] = (codes, scales)
+
+        def project(q):
+            if not 0 <= q < QUADS:
+                return
+            codes, scales = words[q]
+            proj = proj_pool.tile([P, QUAD, WIDTH], F32)
+            for i in range(QUAD):
+                tokens = slice(i * P, (i + 1) * P)
+                nc.tensor.matmul_mx(
+                    out=proj[:, i, :],
+                    lhsT=codes[:, tokens].bitcast(FP8X4),
+                    lhsT_scale=scales[:, tokens],
+                    rhs=w_codes[:].bitcast(FP8X4),
+                    rhs_scale=w_scales[:],
+                    start=True,
+                    stop=True,
+                )
+            projs[q] = proj
+
+        def copy_and_gelu(q):
+            if not 0 <= q < QUADS:
+                return
+            tiles = slice(q * QUAD, (q + 1) * QUAD)
+            qk = out_pool.tile([P, 2, QUAD, QK], F32)
+            nc.scalar.copy(
+                out=qk[:].rearrange("p s i c -> p i s c"),
+                in_=projs[q][:, :, 0 : 2 * QK].rearrange("p i (s c) -> p i s c", s=2),
+            )
+            gelu_pre = out_pool.tile([P, QUAD, EXP], F32)
+            nc.scalar.activation(out=gelu_pre[:], in_=projs[q][:, :, 2 * QK + EXP : WIDTH], func=ACT.Gelu)
+            gelus[q] = gelu_pre
+            nc.sync.dma_start(out=q_rows[:, tiles, :], in_=qk[:, 0, :, :])
+            nc.sync.dma_start(out=k_rows[:, tiles, :], in_=qk[:, 1, :, :])
+
+        def gate(q):
+            if not 0 <= q < QUADS:
+                return
+            tiles = slice(q * QUAD, (q + 1) * QUAD)
+            glv = out_pool.tile([P, 2, QUAD, HALF_EXP], F32)
+            nc.vector.tensor_tensor(
+                out=glv[:].rearrange("p s i c -> p i s c"),
+                in0=projs[q][:, :, 2 * QK : 2 * QK + EXP].rearrange("p i (s c) -> p i s c", s=2),
+                in1=gelus[q][:].rearrange("p i (s c) -> p i s c", s=2),
+                op=ALU.mult,
+            )
+            nc.sync.dma_start(out=gl_rows[:, tiles, :], in_=glv[:, 0, :, :])
+            nc.sync.dma_start(out=gv_rows[:, tiles, :], in_=glv[:, 1, :, :])
+
+        with tc.manual_schedule():
+            for step in range(QUADS + 4):
+                apply_gain(step - 3)
+                normalise(step - 2)
+                inverse_std(step - 1)
+                quantise(step - 3)
+                project(step - 3)
+                sums(step)
+                squares(step)
+                copy_and_gelu(step - 3)
+                gate(step - 4)

@@ -56,7 +56,7 @@ def tile_latentattentionblock_pa_t_kernel(tc, x, norm_w, expand_w, out_0, out_1,
         unread_pool = ctx.enter_context(tc.tile_pool(name="unread", bufs=6))
         y_pool = ctx.enter_context(tc.tile_pool(name="y", bufs=8))
         mx_pool = ctx.enter_context(tc.tile_pool(name="mx", bufs=3))
-        out_pool = ctx.enter_context(tc.tile_pool(name="out", bufs=4))
+        out_pool = ctx.enter_context(tc.tile_pool(name="out", bufs=8))
         turned_pool = ctx.enter_context(tc.psum_pool(name="turned", bufs=6))
         proj_pool = ctx.enter_context(tc.psum_pool(name="proj", bufs=2))
 
@@ -75,6 +75,11 @@ def tile_latentattentionblock_pa_t_kernel(tc, x, norm_w, expand_w, out_0, out_1,
         make_identity(nc, identity[:])
         minus_half = const.tile([P, QUAD], F32)
         nc.vector.memset(minus_half[:], -0.5)
+
+        zero = const.tile([P, 1], F32)
+        nc.vector.memset(zero[:], 0.0)
+        warm = const.tile([P, 1], F32)
+        nc.scalar.activation(out=warm[:], in_=zero[:], func=ACT.Gelu)
 
         gain_rows_f = const.tile([P, P], F32)
         nc.vector.tensor_copy(out=gain_rows_f[:], in_=gain_rows[:])

@@ -60,16 +60,20 @@ def tile_latentattentionblock_pa_t_kernel(tc, x, norm_w, expand_w, out_0, out_1,
         turned_pool = ctx.enter_context(tc.psum_pool(name="turned", bufs=6))
         proj_pool = ctx.enter_context(tc.psum_pool(name="proj", bufs=2))
 
+        x_quads = []
         w_rows = const.tile([P, DIM], BF16)
-        nc.scalar.dma_start(out=w_rows[:], in_=expand_w)
         gain_rows = const.tile([P, P], BF16)
         nc.vector.memset(gain_rows[:], 0.0)
-        nc.scalar.dma_start(out=gain_rows[0:PACK, :].rearrange("j (b r) -> j b r", r=RUN), in_=norm_w.rearrange("(b j r) -> j b r", j=PACK, r=RUN))
-        x_quads = []
         for q in range(QUADS):
             x_quad = x_pool.tile([P, QUAD, DIM], BF16)
             nc.sync.dma_start(out=x_quad[:], in_=x_rows[:, q * QUAD : (q + 1) * QUAD, :])
             x_quads.append(x_quad)
+            if q == 0:
+                nc.sync.dma_start(
+                    out=gain_rows[0:PACK, :].rearrange("j (b r) -> j b r", r=RUN),
+                    in_=norm_w.rearrange("(b j r) -> j b r", j=PACK, r=RUN),
+                )
+                nc.sync.dma_start(out=w_rows[:], in_=expand_w)
 
         identity = const.tile([P, P], F32)
         make_identity(nc, identity[:])
@@ -78,29 +82,27 @@ def tile_latentattentionblock_pa_t_kernel(tc, x, norm_w, expand_w, out_0, out_1,
 
         zero = const.tile([P, 1], F32)
         nc.vector.memset(zero[:], 0.0)
-        warm = const.tile([P, 1], F32)
-        nc.scalar.activation(out=warm[:], in_=zero[:], func=ACT.Gelu)
-
-        gain_rows_f = const.tile([P, P], F32)
-        nc.vector.tensor_copy(out=gain_rows_f[:], in_=gain_rows[:])
-        gain_turned = turned_pool.tile([P, PACK, P], F32, tag="turned")
-        nc.tensor.transpose(gain_turned[:, 0, :], gain_rows_f[:], identity[:])
         gain = const.tile([P, PACK], F32)
-        nc.vector.tensor_copy(out=gain[:], in_=gain_turned[:, 0, 0:PACK])
-
-        w_rows_f = const.tile([P, DIM], F32)
-        nc.vector.tensor_copy(out=slots(w_rows_f[:]), in_=by_slot(w_rows[:]))
-        w_turned = turned_pool.tile([P, PACK, P], F32, tag="turned")
-        turn_rows(nc, w_turned, w_rows_f, identity[:])
-        w_grouped = const.tile([P, P, PACK], BF16, align_bytes=64)
-        nc.vector.tensor_copy(out=w_grouped[:], in_=w_turned[:].rearrange("p j r -> p r j"))
         w_codes = const.tile([P, WIDTH], U32, align_bytes=64)
         w_scales = const.tile([P, WIDTH], U8, align_bytes=64)
-        nc.vector.quantize_mx(
-            out=w_codes[:].bitcast(FP8X4),
-            scales=w_scales[:],
-            in_=w_grouped[:].rearrange("p r j -> p (r j)"),
-        )
+
+        def weights():
+            gain_rows_f = const.tile([P, P], F32)
+            nc.vector.tensor_copy(out=gain_rows_f[:], in_=gain_rows[:])
+            gain_turned = turned_pool.tile([P, PACK, P], F32, tag="turned")
+            nc.tensor.transpose(gain_turned[:, 0, :], gain_rows_f[:], identity[:])
+            w_rows_f = const.tile([P, DIM], F32)
+            nc.vector.tensor_copy(out=slots(w_rows_f[:]), in_=by_slot(w_rows[:]))
+            w_turned = turned_pool.tile([P, PACK, P], F32, tag="turned")
+            turn_rows(nc, w_turned, w_rows_f, identity[:])
+            nc.vector.tensor_copy(out=gain[:], in_=gain_turned[:, 0, 0:PACK])
+            w_grouped = const.tile([P, P, PACK], BF16, align_bytes=64)
+            nc.vector.tensor_copy(out=w_grouped[:], in_=w_turned[:].rearrange("p j r -> p r j"))
+            nc.vector.quantize_mx(
+                out=w_codes[:].bitcast(FP8X4),
+                scales=w_scales[:],
+                in_=w_grouped[:].rearrange("p r j -> p (r j)"),
+            )
 
         minus_means = {}
         square_sums = {}
@@ -255,6 +257,8 @@ def tile_latentattentionblock_pa_t_kernel(tc, x, norm_w, expand_w, out_0, out_1,
             nc.sync.dma_start(out=gv_rows[:, tiles, :], in_=glv[:, 1, :, :])
 
         with tc.manual_schedule():
+            warm = const.tile([P, 1], F32)
+            nc.scalar.activation(out=warm[:], in_=zero[:], func=ACT.Gelu)
             for step in range(QUADS + 4):
                 apply_gain(step - 3)
                 normalise(step - 2)
@@ -265,3 +269,5 @@ def tile_latentattentionblock_pa_t_kernel(tc, x, norm_w, expand_w, out_0, out_1,
                 squares(step)
                 copy_and_gelu(step - 3)
                 gate(step - 4)
+                if step == 0:
+                    weights()

@@ -113,38 +113,50 @@ def tile_latentattentionblock_pa_t_kernel(tc, x, norm_w, expand_w, out_0, out_1,
         projs = {}
         gelus = {}
 
-        def sums(q):
-            if not 0 <= q < QUADS:
-                return
-            by_vector = stat_pool.tile([P, QUAD // 2], F32)
-            by_scalar = stat_pool.tile([P, QUAD // 2], F32)
-            for i in range(QUAD // 2):
-                unread_v = unread_pool.tile([P, DIM], BF16)
-                nc.vector.tensor_scalar(
-                    out=unread_v[:],
-                    in0=x_quads[q][:, i, :],
-                    scalar1=-1.0 / DIM,
-                    scalar2=None,
-                    op0=ALU.mult,
-                    op1=ALU.add,
-                    accum_out=by_vector[:, i : i + 1],
-                )
-                minus_means[(q, i)] = by_vector[:, i : i + 1]
-                unread_s = unread_pool.tile([P, DIM], BF16)
-                nc.scalar.activation(
-                    out=unread_s[:],
-                    in_=x_quads[q][:, QUAD // 2 + i, :],
-                    func=ACT.Identity,
-                    scale=-1.0 / DIM,
-                    accum_out=by_scalar[:, i : i + 1],
-                )
-                minus_means[(q, QUAD // 2 + i)] = by_scalar[:, i : i + 1]
+        def vector_sums(q):
+            return 4 if q < 2 else 1 + (q % 3 == 0)
 
-        def squares(q):
+        def sums(q, vector):
             if not 0 <= q < QUADS:
                 return
-            square_sum = stat_pool.tile([P, QUAD], F32)
-            for i in list(range(QUAD // 2, QUAD)) + list(range(QUAD // 2)):
+            tiles = range(vector_sums(q)) if vector else range(vector_sums(q), QUAD)
+            if vector:
+                by_vector = stat_pool.tile([P, QUAD], F32)
+            elif len(tiles) > 0:
+                by_scalar = stat_pool.tile([P, QUAD], F32)
+            for i in tiles:
+                if vector:
+                    unread_v = unread_pool.tile([P, DIM], BF16)
+                    nc.vector.tensor_scalar(
+                        out=unread_v[:],
+                        in0=x_quads[q][:, i, :],
+                        scalar1=-1.0 / DIM,
+                        scalar2=None,
+                        op0=ALU.mult,
+                        op1=ALU.add,
+                        accum_out=by_vector[:, i : i + 1],
+                    )
+                    minus_means[(q, i)] = by_vector[:, i : i + 1]
+                else:
+                    unread_s = unread_pool.tile([P, DIM], BF16)
+                    nc.scalar.activation(
+                        out=unread_s[:],
+                        in_=x_quads[q][:, i, :],
+                        func=ACT.Identity,
+                        scale=-1.0 / DIM,
+                        accum_out=by_scalar[:, i : i + 1],
+                    )
+                    minus_means[(q, i)] = by_scalar[:, i : i + 1]
+
+        def squares(q, part):
+            if not 0 <= q < QUADS:
+                return
+            if q not in square_sums:
+                square_sums[q] = stat_pool.tile([P, QUAD], F32, name="square_sum")
+            square_sum = square_sums[q]
+            n = vector_sums(q)
+            order = list(range(n, QUAD)) + list(range(n))
+            for i in order[: QUAD // 2] if part == 0 else order[QUAD // 2 :]:
                 unread_s = unread_pool.tile([P, DIM], BF16)
                 nc.scalar.activation(
                     out=unread_s[:],
@@ -153,25 +165,31 @@ def tile_latentattentionblock_pa_t_kernel(tc, x, norm_w, expand_w, out_0, out_1,
                     bias=minus_means[(q, i)],
                     accum_out=square_sum[:, i : i + 1],
                 )
-            square_sums[q] = square_sum
 
-        def inverse_std(q):
+        var_epss = {}
+
+        def variance(q):
             if not 0 <= q < QUADS:
                 return
             var_eps = stat_pool.tile([P, QUAD], F32)
             nc.vector.tensor_scalar(
                 out=var_eps[:], in0=square_sums[q][:], scalar1=1.0 / DIM, scalar2=EPS, op0=ALU.mult, op1=ALU.add
             )
-            rstd = stat_pool.tile([P, QUAD], F32)
-            nc.gpsimd.tensor_tensor(out=rstd[:], in0=var_eps[:], in1=minus_half[:], op=ALU.pow)
-            rstds[q] = rstd
+            var_epss[q] = var_eps
 
-        def normalise(q):
+        def inverse_std(q):
             if not 0 <= q < QUADS:
                 return
-            for i in range(QUAD):
+            rstd = stat_pool.tile([P, QUAD], F32)
+            nc.gpsimd.tensor_tensor(out=rstd[:], in0=var_epss[q][:], in1=minus_half[:], op=ALU.pow)
+            rstds[q] = rstd
+
+        def normalise(q, tiles):
+            if not 0 <= q < QUADS:
+                return
+            for i in tiles:
                 y = y_pool.tile([P, DIM], F32)
-                engine = nc.gpsimd if i % 2 == 0 else nc.vector
+                engine = nc.gpsimd if i == 0 else nc.vector
                 engine.tensor_scalar(
                     out=slots(y[:]),
                     in0=by_slot(x_quads[q][:, i, :]),
@@ -259,15 +277,19 @@ def tile_latentattentionblock_pa_t_kernel(tc, x, norm_w, expand_w, out_0, out_1,
         with tc.manual_schedule():
             warm = const.tile([P, 1], F32)
             nc.scalar.activation(out=warm[:], in_=zero[:], func=ACT.Gelu)
-            for step in range(QUADS + 4):
+            for step in range(QUADS + 5):
+                project(step - 5)
                 apply_gain(step - 3)
-                normalise(step - 2)
+                copy_and_gelu(step - 5)
+                normalise(step - 2, [0])
+                normalise(step - 2, [1, 2, 3])
+                sums(step, False)
+                variance(step - 1)
                 inverse_std(step - 1)
-                quantise(step - 3)
-                project(step - 3)
-                sums(step)
-                squares(step)
-                copy_and_gelu(step - 3)
-                gate(step - 4)
+                quantise(step - 4)
+                sums(step, True)
+                gate(step - 5)
+                squares(step, 0)
+                squares(step, 1)
                 if step == 0:
                     weights()

@@ -57,7 +57,9 @@ def tile_latentattentionblock_pa_t_kernel(tc, x, norm_w, expand_w, out_0, out_1,
         y_pool = ctx.enter_context(tc.tile_pool(name="y", bufs=8))
         mx_pool = ctx.enter_context(tc.tile_pool(name="mx", bufs=3))
         out_pool = ctx.enter_context(tc.tile_pool(name="out", bufs=8))
-        turned_pool = ctx.enter_context(tc.psum_pool(name="turned", bufs=6))
+        xt_sb_pool = ctx.enter_context(tc.tile_pool(name="xts", bufs=4))
+        turned_pool = ctx.enter_context(tc.psum_pool(name="turned", bufs=4))
+        xt_pool = ctx.enter_context(tc.psum_pool(name="xt", bufs=1))
         proj_pool = ctx.enter_context(tc.psum_pool(name="proj", bufs=2))
 
         x_quads = []
@@ -77,6 +79,10 @@ def tile_latentattentionblock_pa_t_kernel(tc, x, norm_w, expand_w, out_0, out_1,
 
         identity = const.tile([P, P], F32)
         make_identity(nc, identity[:])
+        identity_b = const.tile([P, P], BF16)
+        nc.vector.tensor_copy(out=identity_b[:], in_=identity[:])
+        minus_share = const.tile([P, 1], BF16)
+        nc.gpsimd.memset(minus_share[:], -1.0 / DIM)
         minus_half = const.tile([P, QUAD], F32)
         nc.vector.memset(minus_half[:], -0.5)
 
@@ -114,17 +120,74 @@ def tile_latentattentionblock_pa_t_kernel(tc, x, norm_w, expand_w, out_0, out_1,
         gelus = {}
 
         def vector_sums(q):
-            return 4 if q < 2 else 1 + (q % 3 == 0)
+            return 4 if q < 2 else q % 2
+
+        def tensor_sums(q):
+            return 0 if q < 2 else 3
+
+        x_turneds = {}
+        x_fetcheds = {}
+
+        def x_tiles(q, part):
+            if not 0 <= q < QUADS:
+                return []
+            tiles = list(range(vector_sums(q), vector_sums(q) + tensor_sums(q)))
+            return tiles[:-1] if part == 0 else tiles[-1:]
+
+        def turn_x(q, part):
+            tiles = x_tiles(q, part)
+            if not tiles:
+                return
+            bank = xt_pool.tile([P, DIM], F32, tag="xt_%d" % part)
+            turned = bank[:].bitcast(BF16)
+            for n, i in enumerate(tiles):
+                for j in range(PACK):
+                    nc.tensor.transpose(
+                        turned[:, n * DIM + j * P : n * DIM + (j + 1) * P], x_quads[q][:, i, j * P : (j + 1) * P], identity_b[:]
+                    )
+            x_turneds[(q, part)] = bank
+
+        def fetch_x(q, part):
+            n = len(x_tiles(q, part))
+            if n == 0:
+                return
+            fetched = xt_sb_pool.tile([P, 2, DIM], BF16, tag="xts")
+            nc.scalar.copy(
+                out=fetched[:, 0:n, :],
+                in_=x_turneds[(q, part)][:].bitcast(BF16)[:, 0 : n * DIM].rearrange("p (n d) -> p n d", n=n),
+            )
+            x_fetcheds[(q, part)] = fetched
+
+        def sum_x(q, part):
+            for n, i in enumerate(x_tiles(q, part)):
+                c = DIM // 2 + i - vector_sums(q)
+                for j in range(PACK):
+                    nc.tensor.matmul(
+                        out=x_turneds[(q, 1)][:, c : c + 1],
+                        lhsT=x_fetcheds[(q, part)][:, n, j * P : (j + 1) * P],
+                        rhs=minus_share[:],
+                        start=(j == 0),
+                        stop=(j == PACK - 1),
+                    )
+
+        def fetch_sum(q):
+            n = tensor_sums(q) if 0 <= q < QUADS else 0
+            if n == 0:
+                return
+            minus = stat_pool.tile([P, QUAD], F32)
+            first = vector_sums(q)
+            nc.vector.tensor_copy(out=minus[:, 0:n], in_=x_turneds[(q, 1)][:, DIM // 2 : DIM // 2 + n])
+            for k in range(n):
+                minus_means[(q, first + k)] = minus[:, k : k + 1]
 
         def sums(q, vector):
             if not 0 <= q < QUADS:
                 return
-            tiles = range(vector_sums(q)) if vector else range(vector_sums(q), QUAD)
             if vector:
                 by_vector = stat_pool.tile([P, QUAD], F32)
-            elif len(tiles) > 0:
+            elif vector_sums(q) + tensor_sums(q) < QUAD:
                 by_scalar = stat_pool.tile([P, QUAD], F32)
-            for i in tiles:
+            for i in range(vector_sums(q)) if vector else range(vector_sums(q) + tensor_sums(q), QUAD):
                 if vector:
                     unread_v = unread_pool.tile([P, DIM], BF16)
                     nc.vector.tensor_scalar(
@@ -154,8 +217,8 @@ def tile_latentattentionblock_pa_t_kernel(tc, x, norm_w, expand_w, out_0, out_1,
             if q not in square_sums:
                 square_sums[q] = stat_pool.tile([P, QUAD], F32, name="square_sum")
             square_sum = square_sums[q]
-            n = vector_sums(q)
-            order = list(range(n, QUAD)) + list(range(n))
+            n = vector_sums(q) + tensor_sums(q)
+            order = list(range(n, QUAD)) + list(range(vector_sums(q), n)) + list(range(vector_sums(q)))
             for i in order[: QUAD // 2] if part == 0 else order[QUAD // 2 :]:
                 unread_s = unread_pool.tile([P, DIM], BF16)
                 nc.scalar.activation(
@@ -277,19 +340,26 @@ def tile_latentattentionblock_pa_t_kernel(tc, x, norm_w, expand_w, out_0, out_1,
         with tc.manual_schedule():
             warm = const.tile([P, 1], F32)
             nc.scalar.activation(out=warm[:], in_=zero[:], func=ACT.Gelu)
-            for step in range(QUADS + 5):
+            for step in range(-1, QUADS + 5):
                 project(step - 5)
                 apply_gain(step - 3)
+                fetch_sum(step)
+                turn_x(step + 1, 0)
                 copy_and_gelu(step - 5)
+                sums(step, False)
+                sums(step, True)
+                turn_x(step + 1, 1)
                 normalise(step - 2, [0])
                 normalise(step - 2, [1, 2, 3])
-                sums(step, False)
                 variance(step - 1)
                 inverse_std(step - 1)
-                quantise(step - 4)
-                sums(step, True)
-                gate(step - 5)
+                fetch_x(step + 1, 0)
+                fetch_x(step + 1, 1)
                 squares(step, 0)
+                sum_x(step + 1, 0)
+                quantise(step - 4)
+                gate(step - 5)
+                sum_x(step + 1, 1)
                 squares(step, 1)
                 if step == 0:
                     weights()

@@ -60,6 +60,7 @@ def tile_latentattentionblock_pa_t_kernel(tc, x, norm_w, expand_w, out_0, out_1,
         xt_sb_pool = ctx.enter_context(tc.tile_pool(name="xts", bufs=4))
         turned_pool = ctx.enter_context(tc.psum_pool(name="turned", bufs=4))
         xt_pool = ctx.enter_context(tc.psum_pool(name="xt", bufs=1))
+        sum_pool = ctx.enter_context(tc.psum_pool(name="sum", bufs=1))
         proj_pool = ctx.enter_context(tc.psum_pool(name="proj", bufs=2))
 
         x_quads = []
@@ -68,7 +69,11 @@ def tile_latentattentionblock_pa_t_kernel(tc, x, norm_w, expand_w, out_0, out_1,
         nc.vector.memset(gain_rows[:], 0.0)
         for q in range(QUADS):
             x_quad = x_pool.tile([P, QUAD, DIM], BF16)
-            nc.sync.dma_start(out=x_quad[:], in_=x_rows[:, q * QUAD : (q + 1) * QUAD, :])
+            for i in range(0, QUAD, 1 if q == 0 else QUAD):
+                n = 1 if q == 0 else QUAD
+                nc.sync.dma_start(
+                    out=x_quad[:, i : i + n, :], in_=x_rows[:, q * QUAD + i : q * QUAD + i + n, :]
+                )
             x_quads.append(x_quad)
             if q == 0:
                 nc.sync.dma_start(
@@ -120,74 +125,68 @@ def tile_latentattentionblock_pa_t_kernel(tc, x, norm_w, expand_w, out_0, out_1,
         gelus = {}
 
         def vector_sums(q):
-            return 4 if q < 2 else q % 2
+            return 4 if q < 2 else int(q % 4 > 0)
 
         def tensor_sums(q):
-            return 0 if q < 2 else 3
+            return 0 if q < 2 else 2
 
         x_turneds = {}
         x_fetcheds = {}
+        tensor_means = {}
 
-        def x_tiles(q, part):
-            if not 0 <= q < QUADS:
-                return []
-            tiles = list(range(vector_sums(q), vector_sums(q) + tensor_sums(q)))
-            return tiles[:-1] if part == 0 else tiles[-1:]
+        def tensor_tiles(q):
+            return range(vector_sums(q), vector_sums(q) + tensor_sums(q)) if 0 <= q < QUADS else []
 
-        def turn_x(q, part):
-            tiles = x_tiles(q, part)
-            if not tiles:
+        def turn_x(q):
+            if len(tensor_tiles(q)) == 0:
                 return
-            bank = xt_pool.tile([P, DIM], F32, tag="xt_%d" % part)
-            turned = bank[:].bitcast(BF16)
-            for n, i in enumerate(tiles):
+            turned = xt_pool.tile([P, 2, PACK, P], BF16)
+            for n, i in enumerate(tensor_tiles(q)):
                 for j in range(PACK):
-                    nc.tensor.transpose(
-                        turned[:, n * DIM + j * P : n * DIM + (j + 1) * P], x_quads[q][:, i, j * P : (j + 1) * P], identity_b[:]
-                    )
-            x_turneds[(q, part)] = bank
+                    nc.tensor.transpose(turned[:, n, j, :], x_quads[q][:, i, j * P : (j + 1) * P], identity_b[:])
+            x_turneds[q] = turned
 
-        def fetch_x(q, part):
-            n = len(x_tiles(q, part))
-            if n == 0:
+        def fetch_x(q):
+            if len(tensor_tiles(q)) == 0:
                 return
-            fetched = xt_sb_pool.tile([P, 2, DIM], BF16, tag="xts")
-            nc.scalar.copy(
-                out=fetched[:, 0:n, :],
-                in_=x_turneds[(q, part)][:].bitcast(BF16)[:, 0 : n * DIM].rearrange("p (n d) -> p n d", n=n),
-            )
-            x_fetcheds[(q, part)] = fetched
+            fetched = xt_sb_pool.tile([P, 2, PACK, P], BF16)
+            nc.scalar.copy(out=fetched[:], in_=x_turneds[q][:])
+            x_fetcheds[q] = fetched
 
-        def sum_x(q, part):
-            for n, i in enumerate(x_tiles(q, part)):
-                c = DIM // 2 + i - vector_sums(q)
+        def sum_x(q):
+            if len(tensor_tiles(q)) == 0:
+                return
+            means = sum_pool.tile([P, 2], F32)
+            for n in range(len(tensor_tiles(q))):
                 for j in range(PACK):
                     nc.tensor.matmul(
-                        out=x_turneds[(q, 1)][:, c : c + 1],
-                        lhsT=x_fetcheds[(q, part)][:, n, j * P : (j + 1) * P],
+                        out=means[:, n : n + 1],
+                        lhsT=x_fetcheds[q][:, n, j, :],
                         rhs=minus_share[:],
                         start=(j == 0),
                         stop=(j == PACK - 1),
                     )
+            tensor_means[q] = means
 
         def fetch_sum(q):
-            n = tensor_sums(q) if 0 <= q < QUADS else 0
-            if n == 0:
+            if len(tensor_tiles(q)) == 0:
                 return
-            minus = stat_pool.tile([P, QUAD], F32)
-            first = vector_sums(q)
-            nc.vector.tensor_copy(out=minus[:, 0:n], in_=x_turneds[(q, 1)][:, DIM // 2 : DIM // 2 + n])
-            for k in range(n):
-                minus_means[(q, first + k)] = minus[:, k : k + 1]
+            by_tensor = stat_pool.tile([P, 2], F32)
+            nc.vector.tensor_copy(out=by_tensor[:], in_=tensor_means[q][:])
+            for n, i in enumerate(tensor_tiles(q)):
+                minus_means[(q, i)] = by_tensor[:, n : n + 1]
 
         def sums(q, vector):
             if not 0 <= q < QUADS:
                 return
+            tiles = range(vector_sums(q)) if vector else range(vector_sums(q) + tensor_sums(q), QUAD)
+            if len(tiles) == 0:
+                return
             if vector:
                 by_vector = stat_pool.tile([P, QUAD], F32)
-            elif vector_sums(q) + tensor_sums(q) < QUAD:
+            else:
                 by_scalar = stat_pool.tile([P, QUAD], F32)
-            for i in range(vector_sums(q)) if vector else range(vector_sums(q) + tensor_sums(q), QUAD):
+            for i in tiles:
                 if vector:
                     unread_v = unread_pool.tile([P, DIM], BF16)
                     nc.vector.tensor_scalar(
@@ -247,12 +246,18 @@ def tile_latentattentionblock_pa_t_kernel(tc, x, norm_w, expand_w, out_0, out_1,
             nc.gpsimd.tensor_tensor(out=rstd[:], in0=var_epss[q][:], in1=minus_half[:], op=ALU.pow)
             rstds[q] = rstd
 
+        def gpsimd_tiles(q):
+            return [0] if q < QUADS - 1 else []
+
+        def vector_tiles(q):
+            return [i for i in range(QUAD) if i not in gpsimd_tiles(q)]
+
         def normalise(q, tiles):
             if not 0 <= q < QUADS:
                 return
             for i in tiles:
                 y = y_pool.tile([P, DIM], F32)
-                engine = nc.gpsimd if i == 0 else nc.vector
+                engine = nc.gpsimd if i in gpsimd_tiles(q) else nc.vector
                 engine.tensor_scalar(
                     out=slots(y[:]),
                     in0=by_slot(x_quads[q][:, i, :]),
@@ -341,25 +346,22 @@ def tile_latentattentionblock_pa_t_kernel(tc, x, norm_w, expand_w, out_0, out_1,
             warm = const.tile([P, 1], F32)
             nc.scalar.activation(out=warm[:], in_=zero[:], func=ACT.Gelu)
             for step in range(-1, QUADS + 5):
-                project(step - 5)
+                turn_x(step + 1)
                 apply_gain(step - 3)
                 fetch_sum(step)
-                turn_x(step + 1, 0)
                 copy_and_gelu(step - 5)
-                sums(step, False)
-                sums(step, True)
-                turn_x(step + 1, 1)
-                normalise(step - 2, [0])
-                normalise(step - 2, [1, 2, 3])
+                project(step - 4)
+                normalise(step - 2, gpsimd_tiles(step - 2))
+                normalise(step - 2, vector_tiles(step - 2))
                 variance(step - 1)
-                inverse_std(step - 1)
-                fetch_x(step + 1, 0)
-                fetch_x(step + 1, 1)
-                squares(step, 0)
-                sum_x(step + 1, 0)
-                quantise(step - 4)
+                quantise(step - 3)
+                sums(step, False)
                 gate(step - 5)
-                sum_x(step + 1, 1)
+                fetch_x(step + 1)
+                inverse_std(step - 1)
+                sum_x(step + 1)
+                sums(step, True)
+                squares(step, 0)
                 squares(step, 1)
                 if step == 0:
                     weights()

@@ -247,60 +247,75 @@ def tile_latentattentionblock_pa_t_kernel(tc, x, norm_w, expand_w, out_0, out_1,
             rstds[q] = rstd
 
         def gpsimd_tiles(q):
-            return [0] if q < QUADS - 1 else []
+            return [] if q in (0, QUADS - 1) else [0]
+
+        def scalar_tiles(q):
+            return [2, 3] if q == QUADS - 2 else [3] if q == QUADS - 1 else []
 
         def vector_tiles(q):
-            return [i for i in range(QUAD) if i not in gpsimd_tiles(q)]
+            return [i for i in range(QUAD) if i not in gpsimd_tiles(q) + scalar_tiles(q)]
 
         def normalise(q, tiles):
             if not 0 <= q < QUADS:
                 return
             for i in tiles:
                 y = y_pool.tile([P, DIM], F32)
-                engine = nc.gpsimd if i in gpsimd_tiles(q) else nc.vector
-                engine.tensor_scalar(
-                    out=slots(y[:]),
-                    in0=by_slot(x_quads[q][:, i, :]),
-                    scalar1=minus_means[(q, i)],
-                    scalar2=rstds[q][:, i : i + 1],
-                    op0=ALU.add,
-                    op1=ALU.mult,
-                )
+                rstd = rstds[q][:, i : i + 1]
+                if i in scalar_tiles(q):
+                    bias = stat_pool.tile([P, 1], F32)
+                    nc.scalar.activation(out=bias[:], in_=minus_means[(q, i)], func=ACT.Copy, scale=rstd)
+                    nc.scalar.activation(
+                        out=slots(y[:]), in_=by_slot(x_quads[q][:, i, :]), func=ACT.Identity, bias=bias[:], scale=rstd
+                    )
+                else:
+                    engine = nc.gpsimd if i in gpsimd_tiles(q) else nc.vector
+                    engine.tensor_scalar(
+                        out=slots(y[:]),
+                        in0=by_slot(x_quads[q][:, i, :]),
+                        scalar1=minus_means[(q, i)],
+                        scalar2=rstd,
+                        op0=ALU.add,
+                        op1=ALU.mult,
+                    )
                 turned = turned_pool.tile([P, PACK, P], F32, tag="turned")
                 turn_rows(nc, turned, y, identity[:])
                 turneds[(q, i)] = turned
 
-        def apply_gain(q):
+        def apply_gain(q, tiles):
             if not 0 <= q < QUADS:
                 return
-            grouped = mx_pool.tile([P, QUAD, P, PACK], BF16, align_bytes=64)
-            for i in range(QUAD):
+            if q not in groupeds:
+                groupeds[q] = mx_pool.tile([P, QUAD, P, PACK], BF16, align_bytes=64, name="grouped")
+            for i in tiles:
                 nc.vector.tensor_tensor(
-                    out=grouped[:, i, :, :],
+                    out=groupeds[q][:, i, :, :],
                     in0=turneds[(q, i)][:].rearrange("p j r -> p r j"),
                     in1=gain[:].unsqueeze(1).to_broadcast([P, P, PACK]),
                     op=ALU.mult,
                 )
-            groupeds[q] = grouped
 
-        def quantise(q):
+        def quantise(q, tiles):
             if not 0 <= q < QUADS:
                 return
-            codes = mx_pool.tile([P, QUAD * P], U32, align_bytes=64)
-            scales = mx_pool.tile([P, QUAD * P], U8, align_bytes=64)
+            if q not in words:
+                words[q] = (
+                    mx_pool.tile([P, QUAD * P], U32, align_bytes=64, name="codes"),
+                    mx_pool.tile([P, QUAD * P], U8, align_bytes=64, name="scales"),
+                )
+            codes, scales = words[q]
+            tokens = slice(tiles.start * P, tiles.stop * P)
             nc.vector.quantize_mx(
-                out=codes[:].bitcast(FP8X4),
-                scales=scales[:],
-                in_=groupeds[q][:].rearrange("p i r j -> p (i r j)"),
+                out=codes[:, tokens].bitcast(FP8X4),
+                scales=scales[:, tokens],
+                in_=groupeds[q][:, tiles.start : tiles.stop, :, :].rearrange("p i r j -> p (i r j)"),
             )
-            words[q] = (codes, scales)
 
-        def project(q):
+        def project(q, tiles):
             if not 0 <= q < QUADS:
                 return
             codes, scales = words[q]
             proj = proj_pool.tile([P, QUAD, WIDTH], F32)
-            for i in range(QUAD):
+            for i in tiles:
                 tokens = slice(i * P, (i + 1) * P)
                 nc.tensor.matmul_mx(
                     out=proj[:, i, :],
@@ -311,52 +326,61 @@ def tile_latentattentionblock_pa_t_kernel(tc, x, norm_w, expand_w, out_0, out_1,
                     start=True,
                     stop=True,
                 )
-            projs[q] = proj
+            projs[(q, tiles)] = proj
 
-        def copy_and_gelu(q):
+        def copy_and_gelu(q, tiles):
             if not 0 <= q < QUADS:
                 return
-            tiles = slice(q * QUAD, (q + 1) * QUAD)
-            qk = out_pool.tile([P, 2, QUAD, QK], F32)
+            rows = slice(q * QUAD + tiles.start, q * QUAD + tiles.stop)
+            proj = projs[(q, tiles)][:, tiles.start : tiles.stop, :]
+            qk = out_pool.tile([P, 2, len(tiles), QK], F32)
             nc.scalar.copy(
                 out=qk[:].rearrange("p s i c -> p i s c"),
-                in_=projs[q][:, :, 0 : 2 * QK].rearrange("p i (s c) -> p i s c", s=2),
+                in_=proj[:, :, 0 : 2 * QK].rearrange("p i (s c) -> p i s c", s=2),
             )
-            gelu_pre = out_pool.tile([P, QUAD, EXP], F32)
-            nc.scalar.activation(out=gelu_pre[:], in_=projs[q][:, :, 2 * QK + EXP : WIDTH], func=ACT.Gelu)
-            gelus[q] = gelu_pre
-            nc.sync.dma_start(out=q_rows[:, tiles, :], in_=qk[:, 0, :, :])
-            nc.sync.dma_start(out=k_rows[:, tiles, :], in_=qk[:, 1, :, :])
+            gelu_pre = out_pool.tile([P, len(tiles), EXP], F32)
+            nc.scalar.activation(out=gelu_pre[:], in_=proj[:, :, 2 * QK + EXP : WIDTH], func=ACT.Gelu)
+            gelus[(q, tiles)] = gelu_pre
+            nc.sync.dma_start(out=q_rows[:, rows, :], in_=qk[:, 0, :, :])
+            nc.sync.dma_start(out=k_rows[:, rows, :], in_=qk[:, 1, :, :])
 
-        def gate(q):
+        def gate(q, tiles):
             if not 0 <= q < QUADS:
                 return
-            tiles = slice(q * QUAD, (q + 1) * QUAD)
-            glv = out_pool.tile([P, 2, QUAD, HALF_EXP], F32)
+            rows = slice(q * QUAD + tiles.start, q * QUAD + tiles.stop)
+            proj = projs[(q, tiles)][:, tiles.start : tiles.stop, :]
+            glv = out_pool.tile([P, 2, len(tiles), HALF_EXP], F32)
             nc.vector.tensor_tensor(
                 out=glv[:].rearrange("p s i c -> p i s c"),
-                in0=projs[q][:, :, 2 * QK : 2 * QK + EXP].rearrange("p i (s c) -> p i s c", s=2),
-                in1=gelus[q][:].rearrange("p i (s c) -> p i s c", s=2),
+                in0=proj[:, :, 2 * QK : 2 * QK + EXP].rearrange("p i (s c) -> p i s c", s=2),
+                in1=gelus[(q, tiles)][:].rearrange("p i (s c) -> p i s c", s=2),
                 op=ALU.mult,
             )
-            nc.sync.dma_start(out=gl_rows[:, tiles, :], in_=glv[:, 0, :, :])
-            nc.sync.dma_start(out=gv_rows[:, tiles, :], in_=glv[:, 1, :, :])
+            nc.sync.dma_start(out=gl_rows[:, rows, :], in_=glv[:, 0, :, :])
+            nc.sync.dma_start(out=gv_rows[:, rows, :], in_=glv[:, 1, :, :])
+
+        whole = range(QUAD)
+        last = QUADS - 1
+
+        def before_last(q):
+            return q if q < last else QUADS
 
         with tc.manual_schedule():
             warm = const.tile([P, 1], F32)
             nc.scalar.activation(out=warm[:], in_=zero[:], func=ACT.Gelu)
-            for step in range(-1, QUADS + 5):
+            for step in range(-1, QUADS + 3):
                 turn_x(step + 1)
-                apply_gain(step - 3)
-                fetch_sum(step)
-                copy_and_gelu(step - 5)
-                project(step - 4)
+                apply_gain(before_last(step - 3), whole)
+                copy_and_gelu(step - 5, whole)
+                project(step - 4, whole)
                 normalise(step - 2, gpsimd_tiles(step - 2))
                 normalise(step - 2, vector_tiles(step - 2))
+                normalise(step - 2, scalar_tiles(step - 2))
+                fetch_sum(step)
                 variance(step - 1)
-                quantise(step - 3)
+                quantise(before_last(step - 3), whole)
                 sums(step, False)
-                gate(step - 5)
+                gate(step - 5, whole)
                 fetch_x(step + 1)
                 inverse_std(step - 1)
                 sum_x(step + 1)
@@ -365,3 +389,16 @@ def tile_latentattentionblock_pa_t_kernel(tc, x, norm_w, expand_w, out_0, out_1,
                 squares(step, 1)
                 if step == 0:
                     weights()
+            first_half, second_half = range(0, QUAD // 2), range(QUAD // 2, QUAD)
+            apply_gain(last, range(0, QUAD - 1))
+            quantise(last, first_half)
+            project(last, first_half)
+            apply_gain(last, range(QUAD - 1, QUAD))
+            copy_and_gelu(last - 1, whole)
+            copy_and_gelu(last, first_half)
+            gate(last - 1, whole)
+            quantise(last, second_half)
+            project(last, second_half)
+            gate(last, first_half)
+            copy_and_gelu(last, second_half)
+            gate(last, second_half)

from contextlib import ExitStack

import concourse.mybir as mybir
from concourse.masks import make_identity

F32 = mybir.dt.float32
BF16 = mybir.dt.bfloat16
U32 = mybir.dt.uint32
U8 = mybir.dt.uint8
FP8X4 = mybir.dt.float8_e4m3fn_x4
ALU = mybir.AluOpType
ACT = mybir.ActivationFunctionType

P = 128
PACK = 4
RUN = 8
TOKENS = 16 * 1024
DIM = 512
QK = 32
EXP = 32
HALF_EXP = 16
WIDTH = 2 * QK + 2 * EXP
EPS = 1e-5
TILES = TOKENS // P
QUAD = 4
QUADS = TILES // QUAD

FLOPS = 2 * TOKENS * DIM * WIDTH


def by_slot(row):
    return row.rearrange("p (b j r) -> p j b r", j=PACK, r=RUN)


def slots(row):
    return row.rearrange("p (j b r) -> p j b r", j=PACK, r=RUN)


def turn_rows(nc, turned, rows, identity):
    for j in range(PACK):
        nc.tensor.transpose(turned[:, j, :], rows[:, j * P : (j + 1) * P], identity)


def tile_latentattentionblock_pa_t_kernel(tc, x, norm_w, expand_w, out_0, out_1, out_2, out_3):
    nc = tc.nc
    x_rows = x.flatten_outer_dims().rearrange("(p i) d -> p i d", p=P)
    q_rows = out_0.flatten_outer_dims().rearrange("(p i) c -> p i c", p=P)
    k_rows = out_1.flatten_outer_dims().rearrange("(p i) c -> p i c", p=P)
    gl_rows = out_2.flatten_outer_dims().rearrange("(p i) c -> p i c", p=P)
    gv_rows = out_3.flatten_outer_dims().rearrange("(p i) c -> p i c", p=P)

    with ExitStack() as ctx:
        const = ctx.enter_context(tc.tile_pool(name="const", bufs=1))
        x_pool = ctx.enter_context(tc.tile_pool(name="x", bufs=QUADS))
        stat_pool = ctx.enter_context(tc.tile_pool(name="stat", bufs=6))
        unread_pool = ctx.enter_context(tc.tile_pool(name="unread", bufs=6))
        y_pool = ctx.enter_context(tc.tile_pool(name="y", bufs=8))
        mx_pool = ctx.enter_context(tc.tile_pool(name="mx", bufs=3))
        out_pool = ctx.enter_context(tc.tile_pool(name="out", bufs=8))
        xt_sb_pool = ctx.enter_context(tc.tile_pool(name="xts", bufs=4))
        turned_pool = ctx.enter_context(tc.psum_pool(name="turned", bufs=4))
        xt_pool = ctx.enter_context(tc.psum_pool(name="xt", bufs=1))
        sum_pool = ctx.enter_context(tc.psum_pool(name="sum", bufs=1))
        proj_pool = ctx.enter_context(tc.psum_pool(name="proj", bufs=2))

        x_quads = []
        w_rows = const.tile([P, DIM], BF16)
        gain_rows = const.tile([P, P], BF16)
        nc.vector.memset(gain_rows[:], 0.0)
        for q in range(QUADS):
            x_quad = x_pool.tile([P, QUAD, DIM], BF16)
            for i in range(0, QUAD, 1 if q == 0 else QUAD):
                n = 1 if q == 0 else QUAD
                nc.sync.dma_start(
                    out=x_quad[:, i : i + n, :], in_=x_rows[:, q * QUAD + i : q * QUAD + i + n, :]
                )
            x_quads.append(x_quad)
            if q == 0:
                nc.sync.dma_start(
                    out=gain_rows[0:PACK, :].rearrange("j (b r) -> j b r", r=RUN),
                    in_=norm_w.rearrange("(b j r) -> j b r", j=PACK, r=RUN),
                )
                nc.sync.dma_start(out=w_rows[:], in_=expand_w)

        identity = const.tile([P, P], F32)
        make_identity(nc, identity[:])
        identity_b = const.tile([P, P], BF16)
        nc.vector.tensor_copy(out=identity_b[:], in_=identity[:])
        minus_share = const.tile([P, 1], BF16)
        nc.gpsimd.memset(minus_share[:], -1.0 / DIM)
        minus_half = const.tile([P, QUAD], F32)
        nc.vector.memset(minus_half[:], -0.5)

        zero = const.tile([P, 1], F32)
        nc.vector.memset(zero[:], 0.0)
        gain = const.tile([P, PACK], F32)
        w_codes = const.tile([P, WIDTH], U32, align_bytes=64)
        w_scales = const.tile([P, WIDTH], U8, align_bytes=64)

        def weights():
            gain_rows_f = const.tile([P, P], F32)
            nc.vector.tensor_copy(out=gain_rows_f[:], in_=gain_rows[:])
            gain_turned = turned_pool.tile([P, PACK, P], F32, tag="turned")
            nc.tensor.transpose(gain_turned[:, 0, :], gain_rows_f[:], identity[:])
            w_rows_f = const.tile([P, DIM], F32)
            nc.vector.tensor_copy(out=slots(w_rows_f[:]), in_=by_slot(w_rows[:]))
            w_turned = turned_pool.tile([P, PACK, P], F32, tag="turned")
            turn_rows(nc, w_turned, w_rows_f, identity[:])
            nc.vector.tensor_copy(out=gain[:], in_=gain_turned[:, 0, 0:PACK])
            w_grouped = const.tile([P, P, PACK], BF16, align_bytes=64)
            nc.vector.tensor_copy(out=w_grouped[:], in_=w_turned[:].rearrange("p j r -> p r j"))
            nc.vector.quantize_mx(
                out=w_codes[:].bitcast(FP8X4),
                scales=w_scales[:],
                in_=w_grouped[:].rearrange("p r j -> p (r j)"),
            )

        minus_means = {}
        square_sums = {}
        rstds = {}
        turneds = {}
        groupeds = {}
        words = {}
        projs = {}
        gelus = {}

        def vector_sums(q):
            return 4 if q < 2 else int(q % 4 > 0)

        def tensor_sums(q):
            return 0 if q < 2 else 2

        x_turneds = {}
        x_fetcheds = {}
        tensor_means = {}

        def tensor_tiles(q):
            return range(vector_sums(q), vector_sums(q) + tensor_sums(q)) if 0 <= q < QUADS else []

        def turn_x(q):
            if len(tensor_tiles(q)) == 0:
                return
            turned = xt_pool.tile([P, 2, PACK, P], BF16)
            for n, i in enumerate(tensor_tiles(q)):
                for j in range(PACK):
                    nc.tensor.transpose(turned[:, n, j, :], x_quads[q][:, i, j * P : (j + 1) * P], identity_b[:])
            x_turneds[q] = turned

        def fetch_x(q):
            if len(tensor_tiles(q)) == 0:
                return
            fetched = xt_sb_pool.tile([P, 2, PACK, P], BF16)
            nc.scalar.copy(out=fetched[:], in_=x_turneds[q][:])
            x_fetcheds[q] = fetched

        def sum_x(q):
            if len(tensor_tiles(q)) == 0:
                return
            means = sum_pool.tile([P, 2], F32)
            for n in range(len(tensor_tiles(q))):
                for j in range(PACK):
                    nc.tensor.matmul(
                        out=means[:, n : n + 1],
                        lhsT=x_fetcheds[q][:, n, j, :],
                        rhs=minus_share[:],
                        start=(j == 0),
                        stop=(j == PACK - 1),
                    )
            tensor_means[q] = means

        def fetch_sum(q):
            if len(tensor_tiles(q)) == 0:
                return
            by_tensor = stat_pool.tile([P, 2], F32)
            nc.vector.tensor_copy(out=by_tensor[:], in_=tensor_means[q][:])
            for n, i in enumerate(tensor_tiles(q)):
                minus_means[(q, i)] = by_tensor[:, n : n + 1]

        def sums(q, vector):
            if not 0 <= q < QUADS:
                return
            tiles = range(vector_sums(q)) if vector else range(vector_sums(q) + tensor_sums(q), QUAD)
            if len(tiles) == 0:
                return
            if vector:
                by_vector = stat_pool.tile([P, QUAD], F32)
            else:
                by_scalar = stat_pool.tile([P, QUAD], F32)
            for i in tiles:
                if vector:
                    unread_v = unread_pool.tile([P, DIM], BF16)
                    nc.vector.tensor_scalar(
                        out=unread_v[:],
                        in0=x_quads[q][:, i, :],
                        scalar1=-1.0 / DIM,
                        scalar2=None,
                        op0=ALU.mult,
                        op1=ALU.add,
                        accum_out=by_vector[:, i : i + 1],
                    )
                    minus_means[(q, i)] = by_vector[:, i : i + 1]
                else:
                    unread_s = unread_pool.tile([P, DIM], BF16)
                    nc.scalar.activation(
                        out=unread_s[:],
                        in_=x_quads[q][:, i, :],
                        func=ACT.Identity,
                        scale=-1.0 / DIM,
                        accum_out=by_scalar[:, i : i + 1],
                    )
                    minus_means[(q, i)] = by_scalar[:, i : i + 1]

        def squares(q, part):
            if not 0 <= q < QUADS:
                return
            if q not in square_sums:
                square_sums[q] = stat_pool.tile([P, QUAD], F32, name="square_sum")
            square_sum = square_sums[q]
            n = vector_sums(q) + tensor_sums(q)
            order = list(range(n, QUAD)) + list(range(vector_sums(q), n)) + list(range(vector_sums(q)))
            for i in order[: QUAD // 2] if part == 0 else order[QUAD // 2 :]:
                unread_s = unread_pool.tile([P, DIM], BF16)
                nc.scalar.activation(
                    out=unread_s[:],
                    in_=x_quads[q][:, i, :],
                    func=ACT.Square,
                    bias=minus_means[(q, i)],
                    accum_out=square_sum[:, i : i + 1],
                )

        var_epss = {}

        def variance(q):
            if not 0 <= q < QUADS:
                return
            var_eps = stat_pool.tile([P, QUAD], F32)
            nc.vector.tensor_scalar(
                out=var_eps[:], in0=square_sums[q][:], scalar1=1.0 / DIM, scalar2=EPS, op0=ALU.mult, op1=ALU.add
            )
            var_epss[q] = var_eps

        def inverse_std(q):
            if not 0 <= q < QUADS:
                return
            rstd = stat_pool.tile([P, QUAD], F32)
            nc.gpsimd.tensor_tensor(out=rstd[:], in0=var_epss[q][:], in1=minus_half[:], op=ALU.pow)
            rstds[q] = rstd

        def gpsimd_tiles(q):
            return [] if q in (0, QUADS - 1) else [0]

        def scalar_tiles(q):
            return [2, 3] if q == QUADS - 2 else [3] if q == QUADS - 1 else []

        def vector_tiles(q):
            return [i for i in range(QUAD) if i not in gpsimd_tiles(q) + scalar_tiles(q)]

        def normalise(q, tiles):
            if not 0 <= q < QUADS:
                return
            for i in tiles:
                y = y_pool.tile([P, DIM], F32)
                rstd = rstds[q][:, i : i + 1]
                if i in scalar_tiles(q):
                    bias = stat_pool.tile([P, 1], F32)
                    nc.scalar.activation(out=bias[:], in_=minus_means[(q, i)], func=ACT.Copy, scale=rstd)
                    nc.scalar.activation(
                        out=slots(y[:]), in_=by_slot(x_quads[q][:, i, :]), func=ACT.Identity, bias=bias[:], scale=rstd
                    )
                else:
                    engine = nc.gpsimd if i in gpsimd_tiles(q) else nc.vector
                    engine.tensor_scalar(
                        out=slots(y[:]),
                        in0=by_slot(x_quads[q][:, i, :]),
                        scalar1=minus_means[(q, i)],
                        scalar2=rstd,
                        op0=ALU.add,
                        op1=ALU.mult,
                    )
                turned = turned_pool.tile([P, PACK, P], F32, tag="turned")
                turn_rows(nc, turned, y, identity[:])
                turneds[(q, i)] = turned

        def apply_gain(q, tiles):
            if not 0 <= q < QUADS:
                return
            if q not in groupeds:
                groupeds[q] = mx_pool.tile([P, QUAD, P, PACK], BF16, align_bytes=64, name="grouped")
            for i in tiles:
                nc.vector.tensor_tensor(
                    out=groupeds[q][:, i, :, :],
                    in0=turneds[(q, i)][:].rearrange("p j r -> p r j"),
                    in1=gain[:].unsqueeze(1).to_broadcast([P, P, PACK]),
                    op=ALU.mult,
                )

        def quantise(q, tiles):
            if not 0 <= q < QUADS:
                return
            if q not in words:
                words[q] = (
                    mx_pool.tile([P, QUAD * P], U32, align_bytes=64, name="codes"),
                    mx_pool.tile([P, QUAD * P], U8, align_bytes=64, name="scales"),
                )
            codes, scales = words[q]
            tokens = slice(tiles.start * P, tiles.stop * P)
            nc.vector.quantize_mx(
                out=codes[:, tokens].bitcast(FP8X4),
                scales=scales[:, tokens],
                in_=groupeds[q][:, tiles.start : tiles.stop, :, :].rearrange("p i r j -> p (i r j)"),
            )

        def project(q, tiles):
            if not 0 <= q < QUADS:
                return
            codes, scales = words[q]
            proj = proj_pool.tile([P, QUAD, WIDTH], F32)
            for i in tiles:
                tokens = slice(i * P, (i + 1) * P)
                nc.tensor.matmul_mx(
                    out=proj[:, i, :],
                    lhsT=codes[:, tokens].bitcast(FP8X4),
                    lhsT_scale=scales[:, tokens],
                    rhs=w_codes[:].bitcast(FP8X4),
                    rhs_scale=w_scales[:],
                    start=True,
                    stop=True,
                )
            projs[(q, tiles)] = proj

        def copy_and_gelu(q, tiles):
            if not 0 <= q < QUADS:
                return
            rows = slice(q * QUAD + tiles.start, q * QUAD + tiles.stop)
            proj = projs[(q, tiles)][:, tiles.start : tiles.stop, :]
            qk = out_pool.tile([P, 2, len(tiles), QK], F32)
            nc.scalar.copy(
                out=qk[:].rearrange("p s i c -> p i s c"),
                in_=proj[:, :, 0 : 2 * QK].rearrange("p i (s c) -> p i s c", s=2),
            )
            gelu_pre = out_pool.tile([P, len(tiles), EXP], F32)
            nc.scalar.activation(out=gelu_pre[:], in_=proj[:, :, 2 * QK + EXP : WIDTH], func=ACT.Gelu)
            gelus[(q, tiles)] = gelu_pre
            nc.sync.dma_start(out=q_rows[:, rows, :], in_=qk[:, 0, :, :])
            nc.sync.dma_start(out=k_rows[:, rows, :], in_=qk[:, 1, :, :])

        def gate(q, tiles):
            if not 0 <= q < QUADS:
                return
            rows = slice(q * QUAD + tiles.start, q * QUAD + tiles.stop)
            proj = projs[(q, tiles)][:, tiles.start : tiles.stop, :]
            glv = out_pool.tile([P, 2, len(tiles), HALF_EXP], F32)
            nc.vector.tensor_tensor(
                out=glv[:].rearrange("p s i c -> p i s c"),
                in0=proj[:, :, 2 * QK : 2 * QK + EXP].rearrange("p i (s c) -> p i s c", s=2),
                in1=gelus[(q, tiles)][:].rearrange("p i (s c) -> p i s c", s=2),
                op=ALU.mult,
            )
            nc.sync.dma_start(out=gl_rows[:, rows, :], in_=glv[:, 0, :, :])
            nc.sync.dma_start(out=gv_rows[:, rows, :], in_=glv[:, 1, :, :])

        whole = range(QUAD)
        last = QUADS - 1

        def before_last(q):
            return q if q < last else QUADS

        with tc.manual_schedule():
            warm = const.tile([P, 1], F32)
            nc.scalar.activation(out=warm[:], in_=zero[:], func=ACT.Gelu)
            for step in range(-1, QUADS + 3):
                turn_x(step + 1)
                apply_gain(before_last(step - 3), whole)
                copy_and_gelu(step - 5, whole)
                project(step - 4, whole)
                normalise(step - 2, gpsimd_tiles(step - 2))
                normalise(step - 2, vector_tiles(step - 2))
                normalise(step - 2, scalar_tiles(step - 2))
                fetch_sum(step)
                variance(step - 1)
                quantise(before_last(step - 3), whole)
                sums(step, False)
                gate(step - 5, whole)
                fetch_x(step + 1)
                inverse_std(step - 1)
                sum_x(step + 1)
                sums(step, True)
                squares(step, 0)
                squares(step, 1)
                if step == 0:
                    weights()
            first_half, second_half = range(0, QUAD // 2), range(QUAD // 2, QUAD)
            apply_gain(last, range(0, QUAD - 1))
            quantise(last, first_half)
            project(last, first_half)
            apply_gain(last, range(QUAD - 1, QUAD))
            copy_and_gelu(last - 1, whole)
            copy_and_gelu(last, first_half)
            gate(last - 1, whole)
            quantise(last, second_half)
            project(last, second_half)
            gate(last, first_half)
            copy_and_gelu(last, second_half)
            gate(last, second_half)
